import numpy as np
import ml_dtypes


def mxq(x, axis, fmt="e4m3"):
    dtype, down = {"e4m3": (ml_dtypes.float8_e4m3fn, 7), "e5m2": (ml_dtypes.float8_e5m2, 14)}[fmt]
    v = np.moveaxis(np.asarray(x, np.float32).astype(ml_dtypes.bfloat16).astype(np.float64), axis, -1)
    blocks = v.reshape(v.shape[:-1] + (-1, 32))
    amax = np.abs(blocks).max(-1, keepdims=True)
    byte = np.maximum(np.where(amax > 0, np.frexp(amax)[1] - 1 + 127, 0) - down, 1)
    scale = np.exp2(byte - 127.0)
    codes = (blocks / scale).astype(np.float32).astype(dtype).astype(np.float64)
    return np.moveaxis((codes * scale).reshape(v.shape), -1, axis)


WIDE = False


def mx_kscale(k):
    if not WIDE:
        return np.ones(k)
    levels = np.array([20, -20, 10, -10, 0])
    a = np.random.permutation(np.resize(levels, k // 512 * 4)).reshape(k // 512, 4)
    idx = np.arange(k)
    return np.exp2(a[idx // 512, idx % 128 // 32])


BF16 = ml_dtypes.bfloat16


def bf(x):
    return np.asarray(x, np.float32).astype(BF16)


def f64(x):
    return np.asarray(x).astype(np.float64)


B, HH, WW, E, NH, D = 1, 128, 4, 512, 4, 128
KD = NH * D


def setup_inputs():
    u = mx_kscale(E)
    ret_w = np.random.standard_normal((B, HH, WW, NH, D)) * 0.9
    kv_h = np.random.standard_normal((B, WW, NH, D, D)) * 0.8
    Wo = np.random.standard_normal((E, KD)) * 0.3 / np.sqrt(KD) / u[:, None]
    bo = np.random.standard_normal(E) * 0.2
    g = np.random.standard_normal((B, HH * WW, E)) * np.exp2(np.random.randint(-12, 1, (B, HH * WW, 1))) * 8.0 * u
    return {"ret_w": bf(ret_w), "kv_h": bf(kv_h), "Wo": bf(Wo), "bo": bf(bo), "grad_out": bf(g)}


def reference(ret_w, kv_h, Wo, bo, grad_out):
    g = f64(grad_out).reshape(B * HH * WW, E)
    go = mxq(g, 1, "e5m2") @ mxq(f64(Wo), 0, "e4m3")
    go = go.reshape(B, HH, WW * NH, D).transpose(0, 2, 1, 3)
    gr = go @ f64(kv_h).reshape(B, WW * NH, D, D).transpose(0, 1, 3, 2)
    return gr.transpose(0, 2, 1, 3).reshape(B, HH, WW, NH, D)

@@ -1,0 +1,154 @@
+from contextlib import ExitStack
+
+import concourse.mybir as mybir
+from concourse.masks import make_identity
+
+BF16 = mybir.dt.bfloat16
+F32 = mybir.dt.float32
+U32 = mybir.dt.uint32
+U8 = mybir.dt.uint8
+E4M3_X4 = mybir.dt.float8_e4m3fn_x4
+E5M2_X4 = mybir.dt.float8_e5m2_x4
+
+P = 128
+PACK = 4
+HEIGHT, WIDTH, HEADS, D = 128, 4, 4, 128
+E = P * PACK
+KD = HEADS * D
+TOKENS = HEIGHT * WIDTH
+
+FLOPS = 2 * TOKENS * E * KD + 2 * WIDTH * HEADS * HEIGHT * D * D
+BYTES = 2 * (TOKENS * E + E * KD + WIDTH * HEADS * D * D) + 4 * TOKENS * KD
+
+
+def tile_linear_retention_pb_s_kernel(tc, ret_w, kv_h, Wo, bo, grad_out, out):
+    nc = tc.nc
+    with ExitStack() as ctx:
+        keep = ctx.enter_context(tc.tile_pool(name="keep", bufs=1))
+        psum_t = ctx.enter_context(tc.psum_pool(name="psum_t", bufs=2))
+        psum_mx = ctx.enter_context(tc.psum_pool(name="psum_mx", bufs=2))
+        psum_out = ctx.enter_context(tc.psum_pool(name="psum_out", bufs=2))
+
+        g_rows = grad_out[0].rearrange("(h w) k -> h w k", w=WIDTH)
+        g_sb = []
+        for w in range(WIDTH):
+            g_w = keep.tile([HEIGHT, E], BF16, name="g_sb%d" % w)
+            nc.sync.dma_start(out=g_w[:], in_=g_rows[:, w, :])
+            g_sb.append(g_w)
+        wo_raw = keep.tile([P, PACK, KD], BF16, name="wo_raw")
+        nc.sync.dma_start(out=wo_raw[:], in_=Wo.rearrange("(p t) c -> p t c", t=PACK))
+        kv_sb = []
+        for n in range(HEADS):
+            kv_n = keep.tile([D, WIDTH, D], BF16, name="kv_sb%d" % n)
+            nc.sync.dma_start(out=kv_n[:], in_=kv_h[0, :, n].rearrange("w e f -> e w f"))
+            kv_sb.append(kv_n)
+
+        ident_f32 = keep.tile([P, P], F32, name="ident_f32")
+        make_identity(nc, ident_f32[:])
+        ident_bf16 = keep.tile([P, P], BF16, name="ident_bf16")
+        make_identity(nc, ident_bf16[:])
+
+        g_codes = keep.tile([P, TOKENS], U32, name="g_codes", align_bytes=64)
+        g_scales = keep.tile([P, TOKENS], U8, name="g_scales", align_bytes=64)
+        wo_grouped = keep.tile([P, KD, PACK], BF16, name="wo_grouped", align_bytes=64)
+        wo_codes = keep.tile([P, KD], U32, name="wo_codes", align_bytes=64)
+        wo_scales = keep.tile([P, KD], U8, name="wo_scales", align_bytes=64)
+
+        g_grouped = []
+
+        def transpose_g(w):
+            words = g_sb[w][:].bitcast(F32).rearrange("h (p u) -> h u p", u=2)
+            g_t = psum_t.tile([P, 2, HEIGHT], F32, tag="g_t")
+            for u in range(2):
+                nc.tensor.transpose(g_t[:, u, :], words[:, u, :], ident_f32[:])
+            grouped = keep.tile([P, HEIGHT, PACK], BF16, name="g_grouped%d" % w, align_bytes=64)
+            nc.scalar.copy(out=grouped[:].bitcast(F32), in_=g_t[:].rearrange("p u h -> p h u"))
+            g_grouped.append(grouped)
+
+        def quantise_g(w):
+            cols = slice(w * HEIGHT, (w + 1) * HEIGHT)
+            nc.vector.quantize_mx(
+                out=g_codes[:, cols].bitcast(E5M2_X4),
+                scales=g_scales[:, cols],
+                in_=g_grouped[w][:].rearrange("p h t -> p (h t)"),
+            )
+
+        def regroup_wo(n):
+            cols = slice(n * D, (n + 1) * D)
+            nc.vector.tensor_copy(
+                out=wo_grouped[:, cols, :], in_=wo_raw[:, :, cols].rearrange("p t c -> p c t")
+            )
+
+        def quantise_wo(n):
+            cols = slice(n * D, (n + 1) * D)
+            nc.vector.quantize_mx(
+                out=wo_codes[:, cols].bitcast(E4M3_X4),
+                scales=wo_scales[:, cols],
+                in_=wo_grouped[:, cols, :].rearrange("p c t -> p (c t)"),
+            )
+
+        kv_t = []
+
+        def transpose_kv(n):
+            kv_t_ps = psum_t.tile([D, WIDTH, D], BF16, tag="kv_t_ps")
+            for w in range(WIDTH):
+                nc.tensor.transpose(kv_t_ps[:, w, :], kv_sb[n][:, w, :], ident_bf16[:])
+            kv_t_n = keep.tile([D, WIDTH, D], F32, name="kv_t%d" % n)
+            nc.scalar.copy(out=kv_t_n[:], in_=kv_t_ps[:])
+            kv_t.append(kv_t_n)
+
+        go2_t = []
+
+        def first_matmul(n):
+            cols = slice(n * D, (n + 1) * D)
+            go2_ps = psum_mx.tile([D, TOKENS], F32, tag="go2_ps")
+            nc.tensor.matmul_mx(
+                out=go2_ps[:],
+                lhsT=wo_codes[:, cols].bitcast(E4M3_X4),
+                lhsT_scale=wo_scales[:, cols],
+                rhs=g_codes[:].bitcast(E5M2_X4),
+                rhs_scale=g_scales[:],
+                start=True,
+                stop=True,
+            )
+            go2_n = keep.tile([D, TOKENS], F32, name="go2_t%d" % n)
+            nc.vector.tensor_copy(out=go2_n[:], in_=go2_ps[:])
+            go2_t.append(go2_n)
+
+        out_sb = keep.tile([HEIGHT, WIDTH, HEADS, D], F32, name="out_sb")
+
+        def second_matmul(n):
+            for half in range(2):
+                out_ps = psum_out.tile([HEIGHT, 2, D], F32, tag="out_ps")
+                for i in range(2):
+                    w = 2 * half + i
+                    nc.tensor.matmul(
+                        out=out_ps[:, i, :],
+                        lhsT=go2_t[n][:, w * HEIGHT : (w + 1) * HEIGHT],
+                        rhs=kv_t[n][:, w, :],
+                        start=True,
+                        stop=True,
+                    )
+                if half == 0:
+                    nc.scalar.copy(out=out_sb[:, 0:2, n, :], in_=out_ps[:])
+                else:
+                    nc.vector.tensor_copy(out=out_sb[:, 2:4, n, :], in_=out_ps[:])
+            nc.sync.dma_start(out=out[0, :, :, n, :], in_=out_sb[:, :, n, :])
+
+        def prepare(n):
+            if n + 1 < HEADS:
+                regroup_wo(n + 1)
+            quantise_wo(n)
+            transpose_kv(n)
+            first_matmul(n)
+
+        for w in range(WIDTH):
+            transpose_g(w)
+        for w in range(WIDTH):
+            quantise_g(w)
+        regroup_wo(0)
+        prepare(0)
+        for n in range(HEADS):
+            if n + 1 < HEADS:
+                prepare(n + 1)
+            second_matmul(n)

@@ -25,9 +25,8 @@ def tile_linear_retention_pb_s_kernel(tc, ret_w, kv_h, Wo, bo, grad_out, out):
     nc = tc.nc
     with ExitStack() as ctx:
         keep = ctx.enter_context(tc.tile_pool(name="keep", bufs=1))
-        psum_t = ctx.enter_context(tc.psum_pool(name="psum_t", bufs=2))
-        psum_mx = ctx.enter_context(tc.psum_pool(name="psum_mx", bufs=2))
-        psum_out = ctx.enter_context(tc.psum_pool(name="psum_out", bufs=2))
+        psum_mx = ctx.enter_context(tc.psum_pool(name="psum_mx", bufs=HEADS))
+        psum_rot = ctx.enter_context(tc.psum_pool(name="psum_rot", bufs=4))
 
         g_rows = grad_out[0].rearrange("(h w) k -> h w k", w=WIDTH)
         g_sb = []
@@ -58,7 +57,7 @@ def tile_linear_retention_pb_s_kernel(tc, ret_w, kv_h, Wo, bo, grad_out, out):
 
         def transpose_g(w):
             words = g_sb[w][:].bitcast(F32).rearrange("h (p u) -> h u p", u=2)
-            g_t = psum_t.tile([P, 2, HEIGHT], F32, tag="g_t")
+            g_t = psum_rot.tile([P, 2, HEIGHT], F32, tag="rot")
             for u in range(2):
                 nc.tensor.transpose(g_t[:, u, :], words[:, u, :], ident_f32[:])
             grouped = keep.tile([P, HEIGHT, PACK], BF16, name="g_grouped%d" % w, align_bytes=64)
@@ -90,7 +89,7 @@ def tile_linear_retention_pb_s_kernel(tc, ret_w, kv_h, Wo, bo, grad_out, out):
         kv_t = []
 
         def transpose_kv(n):
-            kv_t_ps = psum_t.tile([D, WIDTH, D], BF16, tag="kv_t_ps")
+            kv_t_ps = psum_rot.tile([D, WIDTH, D], BF16, tag="rot")
             for w in range(WIDTH):
                 nc.tensor.transpose(kv_t_ps[:, w, :], kv_sb[n][:, w, :], ident_bf16[:])
             kv_t_n = keep.tile([D, WIDTH, D], F32, name="kv_t%d" % n)
@@ -112,14 +111,17 @@ def tile_linear_retention_pb_s_kernel(tc, ret_w, kv_h, Wo, bo, grad_out, out):
                 stop=True,
             )
             go2_n = keep.tile([D, TOKENS], F32, name="go2_t%d" % n)
-            nc.vector.tensor_copy(out=go2_n[:], in_=go2_ps[:])
+            if n % 2 == 0:
+                nc.vector.tensor_copy(out=go2_n[:], in_=go2_ps[:])
+            else:
+                nc.scalar.copy(out=go2_n[:], in_=go2_ps[:])
             go2_t.append(go2_n)
 
         out_sb = keep.tile([HEIGHT, WIDTH, HEADS, D], F32, name="out_sb")
 
         def second_matmul(n):
             for half in range(2):
-                out_ps = psum_out.tile([HEIGHT, 2, D], F32, tag="out_ps")
+                out_ps = psum_rot.tile([HEIGHT, 2, D], F32, tag="rot")
                 for i in range(2):
                     w = 2 * half + i
                     nc.tensor.matmul(
@@ -135,20 +137,19 @@ def tile_linear_retention_pb_s_kernel(tc, ret_w, kv_h, Wo, bo, grad_out, out):
                     nc.vector.tensor_copy(out=out_sb[:, 2:4, n, :], in_=out_ps[:])
             nc.sync.dma_start(out=out[0, :, :, n, :], in_=out_sb[:, :, n, :])
 
-        def prepare(n):
-            if n + 1 < HEADS:
-                regroup_wo(n + 1)
-            quantise_wo(n)
-            transpose_kv(n)
-            first_matmul(n)
-
-        for w in range(WIDTH):
-            transpose_g(w)
-        for w in range(WIDTH):
-            quantise_g(w)
-        regroup_wo(0)
-        prepare(0)
-        for n in range(HEADS):
-            if n + 1 < HEADS:
-                prepare(n + 1)
-            second_matmul(n)
+        with tc.manual_schedule():
+            for w in range(WIDTH):
+                transpose_g(w)
+            for w in range(WIDTH):
+                quantise_g(w)
+            regroup_wo(0)
+            for n in range(HEADS):
+                if n + 1 < HEADS:
+                    regroup_wo(n + 1)
+                quantise_wo(n)
+            for n in range(HEADS):
+                transpose_kv(n)
+            for n in range(HEADS):
+                first_matmul(n)
+            for n in range(HEADS):
+                second_matmul(n)

@@ -17,6 +17,8 @@ E = P * PACK
 KD = HEADS * D
 TOKENS = HEIGHT * WIDTH
 
+IDLE_MATMULS = 3
+
 FLOPS = 2 * TOKENS * E * KD + 2 * WIDTH * HEADS * HEIGHT * D * D
 BYTES = 2 * (TOKENS * E + E * KD + WIDTH * HEADS * D * D) + 4 * TOKENS * KD
 
@@ -52,6 +54,11 @@ def tile_linear_retention_pb_s_kernel(tc, ret_w, kv_h, Wo, bo, grad_out, out):
         wo_grouped = keep.tile([P, KD, PACK], BF16, name="wo_grouped", align_bytes=64)
         wo_codes = keep.tile([P, KD], U32, name="wo_codes", align_bytes=64)
         wo_scales = keep.tile([P, KD], U8, name="wo_scales", align_bytes=64)
+
+        def idle_matmuls(count):
+            idle_ps = psum_rot.tile([P, P], F32, tag="rot")
+            for i in range(count):
+                nc.tensor.matmul(out=idle_ps[:], lhsT=ident_f32[:], rhs=ident_f32[:], start=True, stop=True)
 
         g_grouped = []
 
@@ -140,6 +147,7 @@ def tile_linear_retention_pb_s_kernel(tc, ret_w, kv_h, Wo, bo, grad_out, out):
         with tc.manual_schedule():
             for w in range(WIDTH):
                 transpose_g(w)
+            idle_matmuls(IDLE_MATMULS)
             for w in range(WIDTH):
                 quantise_g(w)
             regroup_wo(0)

@@ -16,8 +16,7 @@ HEIGHT, WIDTH, HEADS, D = 128, 4, 4, 128
 E = P * PACK
 KD = HEADS * D
 TOKENS = HEIGHT * WIDTH
-
-IDLE_MATMULS = 3
+IDLE_MATMULS = 2
 
 FLOPS = 2 * TOKENS * E * KD + 2 * WIDTH * HEADS * HEIGHT * D * D
 BYTES = 2 * (TOKENS * E + E * KD + WIDTH * HEADS * D * D) + 4 * TOKENS * KD
@@ -39,26 +38,27 @@ def tile_linear_retention_pb_s_kernel(tc, ret_w, kv_h, Wo, bo, grad_out, out):
         wo_raw = keep.tile([P, PACK, KD], BF16, name="wo_raw")
         nc.sync.dma_start(out=wo_raw[:], in_=Wo.rearrange("(p t) c -> p t c", t=PACK))
         kv_sb = []
-        for n in range(HEADS):
-            kv_n = keep.tile([D, WIDTH, D], BF16, name="kv_sb%d" % n)
-            nc.sync.dma_start(out=kv_n[:], in_=kv_h[0, :, n].rearrange("w e f -> e w f"))
-            kv_sb.append(kv_n)
+        for w in range(WIDTH):
+            kv_w = keep.tile([P, 4, D], BF16, name="kv_sb%d" % w)
+            nc.sync.dma_start(out=kv_w[:], in_=kv_h[0, w].rearrange("n (q l) f -> (n q) l f", l=4))
+            kv_sb.append(kv_w)
 
         ident_f32 = keep.tile([P, P], F32, name="ident_f32")
         make_identity(nc, ident_f32[:])
         ident_bf16 = keep.tile([P, P], BF16, name="ident_bf16")
         make_identity(nc, ident_bf16[:])
 
+        def copy_by_turns(i, out_ap, in_ap):
+            if i % 2 == 0:
+                nc.vector.tensor_copy(out=out_ap, in_=in_ap)
+            else:
+                nc.scalar.copy(out=out_ap, in_=in_ap)
+
         g_codes = keep.tile([P, TOKENS], U32, name="g_codes", align_bytes=64)
         g_scales = keep.tile([P, TOKENS], U8, name="g_scales", align_bytes=64)
         wo_grouped = keep.tile([P, KD, PACK], BF16, name="wo_grouped", align_bytes=64)
         wo_codes = keep.tile([P, KD], U32, name="wo_codes", align_bytes=64)
         wo_scales = keep.tile([P, KD], U8, name="wo_scales", align_bytes=64)
-
-        def idle_matmuls(count):
-            idle_ps = psum_rot.tile([P, P], F32, tag="rot")
-            for i in range(count):
-                nc.tensor.matmul(out=idle_ps[:], lhsT=ident_f32[:], rhs=ident_f32[:], start=True, stop=True)
 
         g_grouped = []
 
@@ -71,6 +71,11 @@ def tile_linear_retention_pb_s_kernel(tc, ret_w, kv_h, Wo, bo, grad_out, out):
             nc.scalar.copy(out=grouped[:].bitcast(F32), in_=g_t[:].rearrange("p u h -> p h u"))
             g_grouped.append(grouped)
 
+        def idle_matmuls(count):
+            idle_ps = psum_rot.tile([P, P], F32, tag="rot")
+            for i in range(count):
+                nc.tensor.matmul(out=idle_ps[:], lhsT=ident_f32[:], rhs=ident_f32[:], start=True, stop=True)
+
         def quantise_g(w):
             cols = slice(w * HEIGHT, (w + 1) * HEIGHT)
             nc.vector.quantize_mx(
@@ -81,9 +86,7 @@ def tile_linear_retention_pb_s_kernel(tc, ret_w, kv_h, Wo, bo, grad_out, out):
 
         def regroup_wo(n):
             cols = slice(n * D, (n + 1) * D)
-            nc.vector.tensor_copy(
-                out=wo_grouped[:, cols, :], in_=wo_raw[:, :, cols].rearrange("p t c -> p c t")
-            )
+            copy_by_turns(n, wo_grouped[:, cols, :], wo_raw[:, :, cols].rearrange("p t c -> p c t"))
 
         def quantise_wo(n):
             cols = slice(n * D, (n + 1) * D)
@@ -95,13 +98,13 @@ def tile_linear_retention_pb_s_kernel(tc, ret_w, kv_h, Wo, bo, grad_out, out):
 
         kv_t = []
 
-        def transpose_kv(n):
-            kv_t_ps = psum_rot.tile([D, WIDTH, D], BF16, tag="rot")
-            for w in range(WIDTH):
-                nc.tensor.transpose(kv_t_ps[:, w, :], kv_sb[n][:, w, :], ident_bf16[:])
-            kv_t_n = keep.tile([D, WIDTH, D], F32, name="kv_t%d" % n)
-            nc.scalar.copy(out=kv_t_n[:], in_=kv_t_ps[:])
-            kv_t.append(kv_t_n)
+        def transpose_kv(w):
+            kv_t_ps = psum_rot.tile([D, 4, P], BF16, tag="rot")
+            for l in range(4):
+                nc.tensor.transpose(kv_t_ps[:, l, :], kv_sb[w][:, l, :], ident_bf16[:])
+            kv_t_w = keep.tile([D, P, 4], F32, name="kv_t%d" % w)
+            copy_by_turns(w, kv_t_w[:], kv_t_ps[:].rearrange("f l q -> f q l"))
+            kv_t.append(kv_t_w[:].rearrange("f q l -> f (q l)"))
 
         go2_t = []
 
@@ -118,31 +121,26 @@ def tile_linear_retention_pb_s_kernel(tc, ret_w, kv_h, Wo, bo, grad_out, out):
                 stop=True,
             )
             go2_n = keep.tile([D, TOKENS], F32, name="go2_t%d" % n)
-            if n % 2 == 0:
-                nc.vector.tensor_copy(out=go2_n[:], in_=go2_ps[:])
-            else:
-                nc.scalar.copy(out=go2_n[:], in_=go2_ps[:])
+            copy_by_turns(n, go2_n[:], go2_ps[:])
             go2_t.append(go2_n)
 
         out_sb = keep.tile([HEIGHT, WIDTH, HEADS, D], F32, name="out_sb")
 
-        def second_matmul(n):
+        def second_matmul(w):
             for half in range(2):
                 out_ps = psum_rot.tile([HEIGHT, 2, D], F32, tag="rot")
                 for i in range(2):
-                    w = 2 * half + i
+                    n = 2 * half + i
                     nc.tensor.matmul(
                         out=out_ps[:, i, :],
                         lhsT=go2_t[n][:, w * HEIGHT : (w + 1) * HEIGHT],
-                        rhs=kv_t[n][:, w, :],
+                        rhs=kv_t[w][:, n * D : (n + 1) * D],
                         start=True,
                         stop=True,
                     )
-                if half == 0:
-                    nc.scalar.copy(out=out_sb[:, 0:2, n, :], in_=out_ps[:])
-                else:
-                    nc.vector.tensor_copy(out=out_sb[:, 2:4, n, :], in_=out_ps[:])
-            nc.sync.dma_start(out=out[0, :, :, n, :], in_=out_sb[:, :, n, :])
+                heads = slice(2 * half, 2 * half + 2)
+                copy_by_turns(half, out_sb[:, w, heads, :], out_ps[:])
+                nc.sync.dma_start(out=out[0, :, w, heads, :], in_=out_sb[:, w, heads, :])
 
         with tc.manual_schedule():
             for w in range(WIDTH):
@@ -150,14 +148,13 @@ def tile_linear_retention_pb_s_kernel(tc, ret_w, kv_h, Wo, bo, grad_out, out):
             idle_matmuls(IDLE_MATMULS)
             for w in range(WIDTH):
                 quantise_g(w)
-            regroup_wo(0)
             for n in range(HEADS):
-                if n + 1 < HEADS:
-                    regroup_wo(n + 1)
+                regroup_wo(n)
+            for n in range(HEADS):
                 quantise_wo(n)
-            for n in range(HEADS):
-                transpose_kv(n)
+            for w in range(WIDTH):
+                transpose_kv(w)
             for n in range(HEADS):
                 first_matmul(n)
-            for n in range(HEADS):
-                second_matmul(n)
+            for w in range(WIDTH):
+                second_matmul(w)

@@ -26,8 +26,7 @@ def tile_linear_retention_pb_s_kernel(tc, ret_w, kv_h, Wo, bo, grad_out, out):
     nc = tc.nc
     with ExitStack() as ctx:
         keep = ctx.enter_context(tc.tile_pool(name="keep", bufs=1))
-        psum_mx = ctx.enter_context(tc.psum_pool(name="psum_mx", bufs=HEADS))
-        psum_rot = ctx.enter_context(tc.psum_pool(name="psum_rot", bufs=4))
+        psum = ctx.enter_context(tc.psum_pool(name="psum", bufs=8))
 
         g_rows = grad_out[0].rearrange("(h w) k -> h w k", w=WIDTH)
         g_sb = []
@@ -35,8 +34,12 @@ def tile_linear_retention_pb_s_kernel(tc, ret_w, kv_h, Wo, bo, grad_out, out):
             g_w = keep.tile([HEIGHT, E], BF16, name="g_sb%d" % w)
             nc.sync.dma_start(out=g_w[:], in_=g_rows[:, w, :])
             g_sb.append(g_w)
-        wo_raw = keep.tile([P, PACK, KD], BF16, name="wo_raw")
-        nc.sync.dma_start(out=wo_raw[:], in_=Wo.rearrange("(p t) c -> p t c", t=PACK))
+        wo_rows = Wo.rearrange("(p t) c -> p t c", t=PACK)
+        wo_raw = []
+        for n in range(HEADS):
+            wo_n = keep.tile([P, PACK, D], BF16, name="wo_raw%d" % n)
+            nc.sync.dma_start(out=wo_n[:], in_=wo_rows[:, :, n * D : (n + 1) * D])
+            wo_raw.append(wo_n)
         kv_sb = []
         for w in range(WIDTH):
             kv_w = keep.tile([P, 4, D], BF16, name="kv_sb%d" % w)
@@ -48,8 +51,8 @@ def tile_linear_retention_pb_s_kernel(tc, ret_w, kv_h, Wo, bo, grad_out, out):
         ident_bf16 = keep.tile([P, P], BF16, name="ident_bf16")
         make_identity(nc, ident_bf16[:])
 
-        def copy_by_turns(i, out_ap, in_ap):
-            if i % 2 == 0:
+        def copy_on(engine, out_ap, in_ap):
+            if engine == "vector":
                 nc.vector.tensor_copy(out=out_ap, in_=in_ap)
             else:
                 nc.scalar.copy(out=out_ap, in_=in_ap)
@@ -64,7 +67,7 @@ def tile_linear_retention_pb_s_kernel(tc, ret_w, kv_h, Wo, bo, grad_out, out):
 
         def transpose_g(w):
             words = g_sb[w][:].bitcast(F32).rearrange("h (p u) -> h u p", u=2)
-            g_t = psum_rot.tile([P, 2, HEIGHT], F32, tag="rot")
+            g_t = psum.tile([P, 2, HEIGHT], F32, tag="bank")
             for u in range(2):
                 nc.tensor.transpose(g_t[:, u, :], words[:, u, :], ident_f32[:])
             grouped = keep.tile([P, HEIGHT, PACK], BF16, name="g_grouped%d" % w, align_bytes=64)
@@ -72,7 +75,7 @@ def tile_linear_retention_pb_s_kernel(tc, ret_w, kv_h, Wo, bo, grad_out, out):
             g_grouped.append(grouped)
 
         def idle_matmuls(count):
-            idle_ps = psum_rot.tile([P, P], F32, tag="rot")
+            idle_ps = psum.tile([P, P], F32, tag="bank")
             for i in range(count):
                 nc.tensor.matmul(out=idle_ps[:], lhsT=ident_f32[:], rhs=ident_f32[:], start=True, stop=True)
 
@@ -84,9 +87,9 @@ def tile_linear_retention_pb_s_kernel(tc, ret_w, kv_h, Wo, bo, grad_out, out):
                 in_=g_grouped[w][:].rearrange("p h t -> p (h t)"),
             )
 
-        def regroup_wo(n):
+        def regroup_wo(n, engine):
             cols = slice(n * D, (n + 1) * D)
-            copy_by_turns(n, wo_grouped[:, cols, :], wo_raw[:, :, cols].rearrange("p t c -> p c t"))
+            copy_on(engine, wo_grouped[:, cols, :], wo_raw[n][:].rearrange("p t c -> p c t"))
 
         def quantise_wo(n):
             cols = slice(n * D, (n + 1) * D)
@@ -96,21 +99,26 @@ def tile_linear_retention_pb_s_kernel(tc, ret_w, kv_h, Wo, bo, grad_out, out):
                 in_=wo_grouped[:, cols, :].rearrange("p c t -> p (c t)"),
             )
 
+        kv_t_banks = []
         kv_t = []
 
         def transpose_kv(w):
-            kv_t_ps = psum_rot.tile([D, 4, P], BF16, tag="rot")
+            kv_t_ps = psum.tile([D, 4, P], BF16, tag="bank")
             for l in range(4):
                 nc.tensor.transpose(kv_t_ps[:, l, :], kv_sb[w][:, l, :], ident_bf16[:])
+            kv_t_banks.append(kv_t_ps)
+
+        def copy_kv(w, engine):
             kv_t_w = keep.tile([D, P, 4], F32, name="kv_t%d" % w)
-            copy_by_turns(w, kv_t_w[:], kv_t_ps[:].rearrange("f l q -> f q l"))
+            copy_on(engine, kv_t_w[:], kv_t_banks[w][:].rearrange("f l q -> f q l"))
             kv_t.append(kv_t_w[:].rearrange("f q l -> f (q l)"))
 
-        go2_t = []
+        go2_banks = []
+        go2_t = {}
 
         def first_matmul(n):
             cols = slice(n * D, (n + 1) * D)
-            go2_ps = psum_mx.tile([D, TOKENS], F32, tag="go2_ps")
+            go2_ps = psum.tile([D, TOKENS], F32, tag="bank")
             nc.tensor.matmul_mx(
                 out=go2_ps[:],
                 lhsT=wo_codes[:, cols].bitcast(E4M3_X4),
@@ -120,15 +128,18 @@ def tile_linear_retention_pb_s_kernel(tc, ret_w, kv_h, Wo, bo, grad_out, out):
                 start=True,
                 stop=True,
             )
+            go2_banks.append(go2_ps)
+
+        def copy_go2(n, engine):
             go2_n = keep.tile([D, TOKENS], F32, name="go2_t%d" % n)
-            copy_by_turns(n, go2_n[:], go2_ps[:])
-            go2_t.append(go2_n)
+            copy_on(engine, go2_n[:], go2_banks[n][:])
+            go2_t[n] = go2_n
 
         out_sb = keep.tile([HEIGHT, WIDTH, HEADS, D], F32, name="out_sb")
 
         def second_matmul(w):
             for half in range(2):
-                out_ps = psum_rot.tile([HEIGHT, 2, D], F32, tag="rot")
+                out_ps = psum.tile([HEIGHT, 2, D], F32, tag="bank")
                 for i in range(2):
                     n = 2 * half + i
                     nc.tensor.matmul(
@@ -139,22 +150,37 @@ def tile_linear_retention_pb_s_kernel(tc, ret_w, kv_h, Wo, bo, grad_out, out):
                         stop=True,
                     )
                 heads = slice(2 * half, 2 * half + 2)
-                copy_by_turns(half, out_sb[:, w, heads, :], out_ps[:])
+                copy_on(("scalar", "vector")[half], out_sb[:, w, heads, :], out_ps[:])
                 nc.sync.dma_start(out=out[0, :, w, heads, :], in_=out_sb[:, w, heads, :])
 
         with tc.manual_schedule():
             for w in range(WIDTH):
                 transpose_g(w)
             idle_matmuls(IDLE_MATMULS)
-            for w in range(WIDTH):
+            for w in range(WIDTH - 1):
                 quantise_g(w)
-            for n in range(HEADS):
-                regroup_wo(n)
-            for n in range(HEADS):
-                quantise_wo(n)
+            regroup_wo(0, "vector")
+            quantise_g(WIDTH - 1)
+            regroup_wo(1, "scalar")
+            quantise_wo(0)
+            first_matmul(0)
+            regroup_wo(2, "vector")
+            quantise_wo(1)
+            first_matmul(1)
+            regroup_wo(3, "scalar")
+            quantise_wo(2)
+            first_matmul(2)
+            quantise_wo(3)
+            first_matmul(3)
+            copy_go2(0, "scalar")
+            copy_go2(1, "vector")
             for w in range(WIDTH):
                 transpose_kv(w)
-            for n in range(HEADS):
-                first_matmul(n)
+            copy_kv(0, "scalar")
+            copy_go2(3, "vector")
+            copy_go2(2, "scalar")
+            copy_kv(1, "vector")
+            copy_kv(2, "scalar")
+            copy_kv(3, "vector")
             for w in range(WIDTH):
                 second_matmul(w)

@@ -34,22 +34,18 @@ def tile_linear_retention_pb_s_kernel(tc, ret_w, kv_h, Wo, bo, grad_out, out):
             g_w = keep.tile([HEIGHT, E], BF16, name="g_sb%d" % w)
             nc.sync.dma_start(out=g_w[:], in_=g_rows[:, w, :])
             g_sb.append(g_w)
-        wo_rows = Wo.rearrange("(p t) c -> p t c", t=PACK)
-        wo_raw = []
-        for n in range(HEADS):
-            wo_n = keep.tile([P, PACK, D], BF16, name="wo_raw%d" % n)
-            nc.sync.dma_start(out=wo_n[:], in_=wo_rows[:, :, n * D : (n + 1) * D])
-            wo_raw.append(wo_n)
+        wo_raw = keep.tile([P, PACK, KD], BF16, name="wo_raw")
+        nc.sync.dma_start(out=wo_raw[:], in_=Wo.rearrange("(p t) c -> p t c", t=PACK))
         kv_sb = []
         for w in range(WIDTH):
             kv_w = keep.tile([P, 4, D], BF16, name="kv_sb%d" % w)
             nc.sync.dma_start(out=kv_w[:], in_=kv_h[0, w].rearrange("n (q l) f -> (n q) l f", l=4))
             kv_sb.append(kv_w)
 
-        ident_f32 = keep.tile([P, P], F32, name="ident_f32")
-        make_identity(nc, ident_f32[:])
         ident_bf16 = keep.tile([P, P], BF16, name="ident_bf16")
         make_identity(nc, ident_bf16[:])
+        ident_f32 = keep.tile([P, P], F32, name="ident_f32")
+        make_identity(nc, ident_f32[:])
 
         def copy_on(engine, out_ap, in_ap):
             if engine == "vector":
@@ -89,7 +85,7 @@ def tile_linear_retention_pb_s_kernel(tc, ret_w, kv_h, Wo, bo, grad_out, out):
 
         def regroup_wo(n, engine):
             cols = slice(n * D, (n + 1) * D)
-            copy_on(engine, wo_grouped[:, cols, :], wo_raw[n][:].rearrange("p t c -> p c t"))
+            copy_on(engine, wo_grouped[:, cols, :], wo_raw[:, :, cols].rearrange("p t c -> p c t"))
 
         def quantise_wo(n):
             cols = slice(n * D, (n + 1) * D)
@@ -137,50 +133,52 @@ def tile_linear_retention_pb_s_kernel(tc, ret_w, kv_h, Wo, bo, grad_out, out):
 
         out_sb = keep.tile([HEIGHT, WIDTH, HEADS, D], F32, name="out_sb")
 
-        def second_matmul(w):
-            for half in range(2):
-                out_ps = psum.tile([HEIGHT, 2, D], F32, tag="bank")
-                for i in range(2):
-                    n = 2 * half + i
-                    nc.tensor.matmul(
-                        out=out_ps[:, i, :],
-                        lhsT=go2_t[n][:, w * HEIGHT : (w + 1) * HEIGHT],
-                        rhs=kv_t[w][:, n * D : (n + 1) * D],
-                        start=True,
-                        stop=True,
-                    )
-                heads = slice(2 * half, 2 * half + 2)
-                copy_on(("scalar", "vector")[half], out_sb[:, w, heads, :], out_ps[:])
-                nc.sync.dma_start(out=out[0, :, w, heads, :], in_=out_sb[:, w, heads, :])
+        def second_matmul(w, half, engine):
+            out_ps = psum.tile([HEIGHT, 2, D], F32, tag="bank")
+            for i in range(2):
+                n = 2 * half + i
+                nc.tensor.matmul(
+                    out=out_ps[:, i, :],
+                    lhsT=go2_t[n][:, w * HEIGHT : (w + 1) * HEIGHT],
+                    rhs=kv_t[w][:, n * D : (n + 1) * D],
+                    start=True,
+                    stop=True,
+                )
+            heads = slice(2 * half, 2 * half + 2)
+            copy_on(engine, out_sb[:, w, heads, :], out_ps[:])
+            nc.sync.dma_start(out=out[0, :, w, heads, :], in_=out_sb[:, w, heads, :])
 
         with tc.manual_schedule():
+            idle_matmuls(IDLE_MATMULS)
             for w in range(WIDTH):
                 transpose_g(w)
             idle_matmuls(IDLE_MATMULS)
-            for w in range(WIDTH - 1):
+            for w in range(WIDTH):
                 quantise_g(w)
             regroup_wo(0, "vector")
-            quantise_g(WIDTH - 1)
             regroup_wo(1, "scalar")
-            quantise_wo(0)
-            first_matmul(0)
             regroup_wo(2, "vector")
-            quantise_wo(1)
-            first_matmul(1)
             regroup_wo(3, "scalar")
-            quantise_wo(2)
-            first_matmul(2)
-            quantise_wo(3)
-            first_matmul(3)
-            copy_go2(0, "scalar")
-            copy_go2(1, "vector")
-            for w in range(WIDTH):
-                transpose_kv(w)
+            transpose_kv(0)
+            transpose_kv(1)
+            for n in range(HEADS):
+                quantise_wo(n)
+                first_matmul(n)
+            transpose_kv(2)
+            transpose_kv(3)
             copy_kv(0, "scalar")
+            copy_go2(0, "vector")
+            copy_go2(1, "scalar")
+            copy_go2(2, "vector")
+            copy_kv(1, "scalar")
             copy_go2(3, "vector")
-            copy_go2(2, "scalar")
-            copy_kv(1, "vector")
+            second_matmul(0, 0, "scalar")
             copy_kv(2, "scalar")
             copy_kv(3, "vector")
-            for w in range(WIDTH):
-                second_matmul(w)
+            second_matmul(1, 0, "vector")
+            second_matmul(0, 1, "scalar")
+            second_matmul(1, 1, "vector")
+            second_matmul(2, 0, "scalar")
+            second_matmul(2, 1, "vector")
+            second_matmul(3, 0, "scalar")
+            second_matmul(3, 1, "vector")

@@ -26,7 +26,11 @@ def tile_linear_retention_pb_s_kernel(tc, ret_w, kv_h, Wo, bo, grad_out, out):
     nc = tc.nc
     with ExitStack() as ctx:
         keep = ctx.enter_context(tc.tile_pool(name="keep", bufs=1))
-        psum = ctx.enter_context(tc.psum_pool(name="psum", bufs=8))
+        psum = ctx.enter_context(tc.psum_pool(name="psum", bufs=1))
+
+        def psum_bank(bank, shape, dtype):
+            in_bank = psum.tile(shape, dtype, tag="bank%d" % bank)
+            return in_bank
 
         g_rows = grad_out[0].rearrange("(h w) k -> h w k", w=WIDTH)
         g_sb = []
@@ -63,7 +67,7 @@ def tile_linear_retention_pb_s_kernel(tc, ret_w, kv_h, Wo, bo, grad_out, out):
 
         def transpose_g(w):
             words = g_sb[w][:].bitcast(F32).rearrange("h (p u) -> h u p", u=2)
-            g_t = psum.tile([P, 2, HEIGHT], F32, tag="bank")
+            g_t = psum_bank(w, [P, 2, HEIGHT], F32)
             for u in range(2):
                 nc.tensor.transpose(g_t[:, u, :], words[:, u, :], ident_f32[:])
             grouped = keep.tile([P, HEIGHT, PACK], BF16, name="g_grouped%d" % w, align_bytes=64)
@@ -71,7 +75,7 @@ def tile_linear_retention_pb_s_kernel(tc, ret_w, kv_h, Wo, bo, grad_out, out):
             g_grouped.append(grouped)
 
         def idle_matmuls(count):
-            idle_ps = psum.tile([P, P], F32, tag="bank")
+            idle_ps = psum_bank(7, [P, P], F32)
             for i in range(count):
                 nc.tensor.matmul(out=idle_ps[:], lhsT=ident_f32[:], rhs=ident_f32[:], start=True, stop=True)
 
@@ -95,26 +99,26 @@ def tile_linear_retention_pb_s_kernel(tc, ret_w, kv_h, Wo, bo, grad_out, out):
                 in_=wo_grouped[:, cols, :].rearrange("p c t -> p (c t)"),
             )
 
-        kv_t_banks = []
-        kv_t = []
+        kv_t_banks = {}
+        kv_t = {}
 
         def transpose_kv(w):
-            kv_t_ps = psum.tile([D, 4, P], BF16, tag="bank")
+            kv_t_ps = psum_bank(4 + w, [D, 4, P], BF16)
             for l in range(4):
                 nc.tensor.transpose(kv_t_ps[:, l, :], kv_sb[w][:, l, :], ident_bf16[:])
-            kv_t_banks.append(kv_t_ps)
+            kv_t_banks[w] = kv_t_ps
 
         def copy_kv(w, engine):
             kv_t_w = keep.tile([D, P, 4], F32, name="kv_t%d" % w)
             copy_on(engine, kv_t_w[:], kv_t_banks[w][:].rearrange("f l q -> f q l"))
-            kv_t.append(kv_t_w[:].rearrange("f q l -> f (q l)"))
+            kv_t[w] = kv_t_w[:].rearrange("f q l -> f (q l)")
 
-        go2_banks = []
+        go2_banks = {}
         go2_t = {}
 
         def first_matmul(n):
             cols = slice(n * D, (n + 1) * D)
-            go2_ps = psum.tile([D, TOKENS], F32, tag="bank")
+            go2_ps = psum_bank(n, [D, TOKENS], F32)
             nc.tensor.matmul_mx(
                 out=go2_ps[:],
                 lhsT=wo_codes[:, cols].bitcast(E4M3_X4),
@@ -124,19 +128,23 @@ def tile_linear_retention_pb_s_kernel(tc, ret_w, kv_h, Wo, bo, grad_out, out):
                 start=True,
                 stop=True,
             )
-            go2_banks.append(go2_ps)
+            go2_banks[n] = go2_ps
 
-        def copy_go2(n, engine):
+        for n in range(HEADS):
             go2_n = keep.tile([D, TOKENS], F32, name="go2_t%d" % n)
-            copy_on(engine, go2_n[:], go2_banks[n][:])
             go2_t[n] = go2_n
 
-        out_sb = keep.tile([HEIGHT, WIDTH, HEADS, D], F32, name="out_sb")
+        def copy_go2(n, part, engine):
+            cols = slice(part * 2 * HEIGHT, (part + 1) * 2 * HEIGHT)
+            copy_on(engine, go2_t[n][:, cols], go2_banks[n][:, cols])
 
-        def second_matmul(w, half, engine):
-            out_ps = psum.tile([HEIGHT, 2, D], F32, tag="bank")
-            for i in range(2):
-                n = 2 * half + i
+        out_sb = keep.tile([HEIGHT, WIDTH, HEADS, D], F32, name="out_sb")
+        out_banks = {}
+
+        def second_matmul(w, first_head, heads, bank):
+            out_ps = psum_bank(bank, [HEIGHT, heads, D], F32)
+            for i in range(heads):
+                n = first_head + i
                 nc.tensor.matmul(
                     out=out_ps[:, i, :],
                     lhsT=go2_t[n][:, w * HEIGHT : (w + 1) * HEIGHT],
@@ -144,9 +152,12 @@ def tile_linear_retention_pb_s_kernel(tc, ret_w, kv_h, Wo, bo, grad_out, out):
                     start=True,
                     stop=True,
                 )
-            heads = slice(2 * half, 2 * half + 2)
-            copy_on(engine, out_sb[:, w, heads, :], out_ps[:])
-            nc.sync.dma_start(out=out[0, :, w, heads, :], in_=out_sb[:, w, heads, :])
+            out_banks[(w, first_head)] = out_ps
+
+        def store_out(w, first_head, heads, engine):
+            which = slice(first_head, first_head + heads)
+            copy_on(engine, out_sb[:, w, which, :], out_banks[(w, first_head)][:])
+            nc.sync.dma_start(out=out[0, :, w, which, :], in_=out_sb[:, w, which, :])
 
         with tc.manual_schedule():
             idle_matmuls(IDLE_MATMULS)
@@ -159,26 +170,38 @@ def tile_linear_retention_pb_s_kernel(tc, ret_w, kv_h, Wo, bo, grad_out, out):
             regroup_wo(1, "scalar")
             regroup_wo(2, "vector")
             regroup_wo(3, "scalar")
-            transpose_kv(0)
-            transpose_kv(1)
+            for w in range(WIDTH):
+                transpose_kv(w)
             for n in range(HEADS):
                 quantise_wo(n)
                 first_matmul(n)
-            transpose_kv(2)
-            transpose_kv(3)
             copy_kv(0, "scalar")
-            copy_go2(0, "vector")
-            copy_go2(1, "scalar")
-            copy_go2(2, "vector")
+            copy_go2(0, 0, "scalar")
+            copy_go2(1, 0, "vector")
+            second_matmul(0, 0, 2, 4)
             copy_kv(1, "scalar")
-            copy_go2(3, "vector")
-            second_matmul(0, 0, "scalar")
+            second_matmul(1, 0, 2, 5)
+            copy_go2(2, 0, "vector")
+            copy_go2(3, 0, "vector")
             copy_kv(2, "scalar")
+            second_matmul(0, 2, 2, 6)
             copy_kv(3, "vector")
-            second_matmul(1, 0, "vector")
-            second_matmul(0, 1, "scalar")
-            second_matmul(1, 1, "vector")
-            second_matmul(2, 0, "scalar")
-            second_matmul(2, 1, "vector")
-            second_matmul(3, 0, "scalar")
-            second_matmul(3, 1, "vector")
+            second_matmul(1, 2, 2, 7)
+            store_out(0, 0, 2, "scalar")
+            copy_go2(0, 1, "scalar")
+            copy_go2(1, 1, "scalar")
+            second_matmul(2, 0, 2, 4)
+            store_out(1, 0, 2, "vector")
+            copy_go2(2, 1, "vector")
+            copy_go2(3, 1, "vector")
+            second_matmul(2, 2, 2, 5)
+            store_out(0, 2, 2, "scalar")
+            second_matmul(3, 0, 2, 6)
+            store_out(1, 2, 2, "vector")
+            second_matmul(3, 2, 1, 7)
+            store_out(2, 0, 2, "scalar")
+            second_matmul(3, 3, 1, 4)
+            store_out(2, 2, 2, "vector")
+            store_out(3, 0, 2, "scalar")
+            store_out(3, 2, 1, "vector")
+            store_out(3, 3, 1, "scalar")

@@ -16,6 +16,7 @@ HEIGHT, WIDTH, HEADS, D = 128, 4, 4, 128
 E = P * PACK
 KD = HEADS * D
 TOKENS = HEIGHT * WIDTH
+KV_ROWS = 8
 IDLE_MATMULS = 2
 
 FLOPS = 2 * TOKENS * E * KD + 2 * WIDTH * HEADS * HEIGHT * D * D
@@ -34,17 +35,20 @@ def tile_linear_retention_pb_s_kernel(tc, ret_w, kv_h, Wo, bo, grad_out, out):
 
         g_rows = grad_out[0].rearrange("(h w) k -> h w k", w=WIDTH)
         g_sb = []
-        for w in range(WIDTH):
-            g_w = keep.tile([HEIGHT, E], BF16, name="g_sb%d" % w)
-            nc.sync.dma_start(out=g_w[:], in_=g_rows[:, w, :])
-            g_sb.append(g_w)
+        for pair in range(WIDTH // 2):
+            g_pair = keep.tile([HEIGHT, 2, E], BF16, name="g_sb%d" % pair)
+            nc.sync.dma_start(out=g_pair[:], in_=g_rows[:, 2 * pair : 2 * pair + 2, :])
+            g_sb.append(g_pair)
         wo_raw = keep.tile([P, PACK, KD], BF16, name="wo_raw")
         nc.sync.dma_start(out=wo_raw[:], in_=Wo.rearrange("(p t) c -> p t c", t=PACK))
         kv_sb = []
-        for w in range(WIDTH):
-            kv_w = keep.tile([P, 4, D], BF16, name="kv_sb%d" % w)
-            nc.sync.dma_start(out=kv_w[:], in_=kv_h[0, w].rearrange("n (q l) f -> (n q) l f", l=4))
-            kv_sb.append(kv_w)
+        for pair in range(WIDTH // 2):
+            kv_pair = keep.tile([P, KV_ROWS, D], BF16, name="kv_sb%d" % pair)
+            nc.sync.dma_start(
+                out=kv_pair[:],
+                in_=kv_h[0, 2 * pair : 2 * pair + 2].rearrange("w n (q l) f -> (w n q) l f", l=KV_ROWS),
+            )
+            kv_sb.append(kv_pair)
 
         ident_bf16 = keep.tile([P, P], BF16, name="ident_bf16")
         make_identity(nc, ident_bf16[:])
@@ -66,7 +70,7 @@ def tile_linear_retention_pb_s_kernel(tc, ret_w, kv_h, Wo, bo, grad_out, out):
         g_grouped = []
 
         def transpose_g(w):
-            words = g_sb[w][:].bitcast(F32).rearrange("h (p u) -> h u p", u=2)
+            words = g_sb[w // 2][:, w % 2, :].bitcast(F32).rearrange("h (p u) -> h u p", u=2)
             g_t = psum_bank(w, [P, 2, HEIGHT], F32)
             for u in range(2):
                 nc.tensor.transpose(g_t[:, u, :], words[:, u, :], ident_f32[:])
@@ -100,18 +104,23 @@ def tile_linear_retention_pb_s_kernel(tc, ret_w, kv_h, Wo, bo, grad_out, out):
             )
 
         kv_t_banks = {}
-        kv_t = {}
+        kv_t = []
+        for pair in range(WIDTH // 2):
+            kv_t_pair = keep.tile([D, P, KV_ROWS], F32, name="kv_t%d" % pair)
+            kv_t.append(kv_t_pair)
 
-        def transpose_kv(w):
-            kv_t_ps = psum_bank(4 + w, [D, 4, P], BF16)
-            for l in range(4):
-                nc.tensor.transpose(kv_t_ps[:, l, :], kv_sb[w][:, l, :], ident_bf16[:])
-            kv_t_banks[w] = kv_t_ps
+        def transpose_kv(pair, part):
+            kv_t_ps = psum_bank(4 + 2 * pair + part, [D, 4, P], BF16)
+            for i in range(4):
+                nc.tensor.transpose(kv_t_ps[:, i, :], kv_sb[pair][:, 4 * part + i, :], ident_bf16[:])
+            kv_t_banks[(pair, part)] = kv_t_ps
 
-        def copy_kv(w, engine):
-            kv_t_w = keep.tile([D, P, 4], F32, name="kv_t%d" % w)
-            copy_on(engine, kv_t_w[:], kv_t_banks[w][:].rearrange("f l q -> f q l"))
-            kv_t[w] = kv_t_w[:].rearrange("f q l -> f (q l)")
+        def copy_kv(pair, part, engine):
+            copy_on(
+                engine,
+                kv_t[pair][:, :, 4 * part : 4 * part + 4],
+                kv_t_banks[(pair, part)][:].rearrange("f l q -> f q l"),
+            )
 
         go2_banks = {}
         go2_t = {}
@@ -148,7 +157,7 @@ def tile_linear_retention_pb_s_kernel(tc, ret_w, kv_h, Wo, bo, grad_out, out):
                 nc.tensor.matmul(
                     out=out_ps[:, i, :],
                     lhsT=go2_t[n][:, w * HEIGHT : (w + 1) * HEIGHT],
-                    rhs=kv_t[w][:, n * D : (n + 1) * D],
+                    rhs=kv_t[w // 2][:].rearrange("f q l -> f (q l)")[:, ((w % 2) * HEADS + n) * D : ((w % 2) * HEADS + n + 1) * D],
                     start=True,
                     stop=True,
                 )
@@ -170,22 +179,23 @@ def tile_linear_retention_pb_s_kernel(tc, ret_w, kv_h, Wo, bo, grad_out, out):
             regroup_wo(1, "scalar")
             regroup_wo(2, "vector")
             regroup_wo(3, "scalar")
-            for w in range(WIDTH):
-                transpose_kv(w)
+            for pair in range(WIDTH // 2):
+                for part in range(2):
+                    transpose_kv(pair, part)
             for n in range(HEADS):
                 quantise_wo(n)
                 first_matmul(n)
-            copy_kv(0, "scalar")
+            copy_kv(0, 0, "scalar")
+            copy_kv(0, 1, "scalar")
             copy_go2(0, 0, "scalar")
             copy_go2(1, 0, "vector")
             second_matmul(0, 0, 2, 4)
-            copy_kv(1, "scalar")
             second_matmul(1, 0, 2, 5)
             copy_go2(2, 0, "vector")
             copy_go2(3, 0, "vector")
-            copy_kv(2, "scalar")
+            copy_kv(1, 0, "scalar")
             second_matmul(0, 2, 2, 6)
-            copy_kv(3, "vector")
+            copy_kv(1, 1, "vector")
             second_matmul(1, 2, 2, 7)
             store_out(0, 0, 2, "scalar")
             copy_go2(0, 1, "scalar")

@@ -93,7 +93,11 @@ def tile_linear_retention_pb_s_kernel(tc, ret_w, kv_h, Wo, bo, grad_out, out):
 
         def regroup_wo(n, engine):
             cols = slice(n * D, (n + 1) * D)
-            copy_on(engine, wo_grouped[:, cols, :], wo_raw[:, :, cols].rearrange("p t c -> p c t"))
+            copy_on(
+                engine,
+                wo_grouped[:, cols, :].rearrange("p (c i) t -> p c t i", i=4),
+                wo_raw[:, :, cols].rearrange("p t (c i) -> p c t i", i=4),
+            )
 
         def quantise_wo(n):
             cols = slice(n * D, (n + 1) * D)

@@ -16,7 +16,7 @@ HEIGHT, WIDTH, HEADS, D = 128, 4, 4, 128
 E = P * PACK
 KD = HEADS * D
 TOKENS = HEIGHT * WIDTH
-KV_ROWS = 8
+KV_PIECES = ((0, 2), (2, 1), (3, 1))
 IDLE_MATMULS = 2
 
 FLOPS = 2 * TOKENS * E * KD + 2 * WIDTH * HEADS * HEIGHT * D * D
@@ -42,13 +42,13 @@ def tile_linear_retention_pb_s_kernel(tc, ret_w, kv_h, Wo, bo, grad_out, out):
         wo_raw = keep.tile([P, PACK, KD], BF16, name="wo_raw")
         nc.sync.dma_start(out=wo_raw[:], in_=Wo.rearrange("(p t) c -> p t c", t=PACK))
         kv_sb = []
-        for pair in range(WIDTH // 2):
-            kv_pair = keep.tile([P, KV_ROWS, D], BF16, name="kv_sb%d" % pair)
+        for first_w, count in KV_PIECES:
+            kv_piece = keep.tile([P, 4 * count, D], BF16, name="kv_sb%d" % first_w)
             nc.sync.dma_start(
-                out=kv_pair[:],
-                in_=kv_h[0, 2 * pair : 2 * pair + 2].rearrange("w n (q l) f -> (w n q) l f", l=KV_ROWS),
+                out=kv_piece[:],
+                in_=kv_h[0, first_w : first_w + count].rearrange("w n (q l) f -> (w n q) l f", l=4 * count),
             )
-            kv_sb.append(kv_pair)
+            kv_sb.append(kv_piece)
 
         ident_bf16 = keep.tile([P, P], BF16, name="ident_bf16")
         make_identity(nc, ident_bf16[:])
@@ -109,21 +109,24 @@ def tile_linear_retention_pb_s_kernel(tc, ret_w, kv_h, Wo, bo, grad_out, out):
 
         kv_t_banks = {}
         kv_t = []
-        for pair in range(WIDTH // 2):
-            kv_t_pair = keep.tile([D, P, KV_ROWS], F32, name="kv_t%d" % pair)
-            kv_t.append(kv_t_pair)
+        kv_t_of_w = {}
+        for first_w, count in KV_PIECES:
+            kv_t_piece = keep.tile([D, P, 4 * count], F32, name="kv_t%d" % first_w)
+            kv_t.append(kv_t_piece)
+            for i in range(count):
+                kv_t_of_w[first_w + i] = kv_t_piece[:].rearrange("f q l -> f (q l)")[:, i * KD : (i + 1) * KD]
 
-        def transpose_kv(pair, part):
-            kv_t_ps = psum_bank(4 + 2 * pair + part, [D, 4, P], BF16)
+        def transpose_kv(piece, part, bank):
+            kv_t_ps = psum_bank(bank, [D, 4, P], BF16)
             for i in range(4):
-                nc.tensor.transpose(kv_t_ps[:, i, :], kv_sb[pair][:, 4 * part + i, :], ident_bf16[:])
-            kv_t_banks[(pair, part)] = kv_t_ps
+                nc.tensor.transpose(kv_t_ps[:, i, :], kv_sb[piece][:, 4 * part + i, :], ident_bf16[:])
+            kv_t_banks[(piece, part)] = kv_t_ps
 
-        def copy_kv(pair, part, engine):
+        def copy_kv(piece, part, engine):
             copy_on(
                 engine,
-                kv_t[pair][:, :, 4 * part : 4 * part + 4],
-                kv_t_banks[(pair, part)][:].rearrange("f l q -> f q l"),
+                kv_t[piece][:, :, 4 * part : 4 * part + 4],
+                kv_t_banks[(piece, part)][:].rearrange("f l q -> f q l"),
             )
 
         go2_banks = {}
@@ -161,7 +164,7 @@ def tile_linear_retention_pb_s_kernel(tc, ret_w, kv_h, Wo, bo, grad_out, out):
                 nc.tensor.matmul(
                     out=out_ps[:, i, :],
                     lhsT=go2_t[n][:, w * HEIGHT : (w + 1) * HEIGHT],
-                    rhs=kv_t[w // 2][:].rearrange("f q l -> f (q l)")[:, ((w % 2) * HEADS + n) * D : ((w % 2) * HEADS + n + 1) * D],
+                    rhs=kv_t_of_w[w][:, n * D : (n + 1) * D],
                     start=True,
                     stop=True,
                 )
@@ -183,14 +186,15 @@ def tile_linear_retention_pb_s_kernel(tc, ret_w, kv_h, Wo, bo, grad_out, out):
             regroup_wo(1, "scalar")
             regroup_wo(2, "vector")
             regroup_wo(3, "scalar")
-            for pair in range(WIDTH // 2):
-                for part in range(2):
-                    transpose_kv(pair, part)
+            transpose_kv(0, 0, 4)
+            transpose_kv(0, 1, 5)
+            transpose_kv(1, 0, 6)
+            transpose_kv(2, 0, 7)
             for n in range(HEADS):
                 quantise_wo(n)
                 first_matmul(n)
             copy_kv(0, 0, "scalar")
-            copy_kv(0, 1, "scalar")
+            copy_kv(0, 1, "vector")
             copy_go2(0, 0, "scalar")
             copy_go2(1, 0, "vector")
             second_matmul(0, 0, 2, 4)
@@ -199,7 +203,7 @@ def tile_linear_retention_pb_s_kernel(tc, ret_w, kv_h, Wo, bo, grad_out, out):
             copy_go2(3, 0, "vector")
             copy_kv(1, 0, "scalar")
             second_matmul(0, 2, 2, 6)
-            copy_kv(1, 1, "vector")
+            copy_kv(2, 0, "vector")
             second_matmul(1, 2, 2, 7)
             store_out(0, 0, 2, "scalar")
             copy_go2(0, 1, "scalar")

@@ -69,13 +69,13 @@ def tile_linear_retention_pb_s_kernel(tc, ret_w, kv_h, Wo, bo, grad_out, out):
 
         g_grouped = []
 
-        def transpose_g(w):
+        def transpose_g(w, engine):
             words = g_sb[w // 2][:, w % 2, :].bitcast(F32).rearrange("h (p u) -> h u p", u=2)
             g_t = psum_bank(w, [P, 2, HEIGHT], F32)
             for u in range(2):
                 nc.tensor.transpose(g_t[:, u, :], words[:, u, :], ident_f32[:])
             grouped = keep.tile([P, HEIGHT, PACK], BF16, name="g_grouped%d" % w, align_bytes=64)
-            nc.scalar.copy(out=grouped[:].bitcast(F32), in_=g_t[:].rearrange("p u h -> p h u"))
+            copy_on(engine, grouped[:].bitcast(F32), g_t[:].rearrange("p u h -> p h u"))
             g_grouped.append(grouped)
 
         def idle_matmuls(count):
@@ -150,8 +150,8 @@ def tile_linear_retention_pb_s_kernel(tc, ret_w, kv_h, Wo, bo, grad_out, out):
             go2_n = keep.tile([D, TOKENS], F32, name="go2_t%d" % n)
             go2_t[n] = go2_n
 
-        def copy_go2(n, part, engine):
-            cols = slice(part * 2 * HEIGHT, (part + 1) * 2 * HEIGHT)
+        def copy_go2(n, first_w, count, engine):
+            cols = slice(first_w * HEIGHT, (first_w + count) * HEIGHT)
             copy_on(engine, go2_t[n][:, cols], go2_banks[n][:, cols])
 
         out_sb = keep.tile([HEIGHT, WIDTH, HEADS, D], F32, name="out_sb")
@@ -177,14 +177,18 @@ def tile_linear_retention_pb_s_kernel(tc, ret_w, kv_h, Wo, bo, grad_out, out):
 
         with tc.manual_schedule():
             idle_matmuls(IDLE_MATMULS)
-            for w in range(WIDTH):
-                transpose_g(w)
+            transpose_g(0, "scalar")
+            transpose_g(1, "vector")
+            transpose_g(2, "scalar")
+            transpose_g(3, "scalar")
             idle_matmuls(IDLE_MATMULS)
-            for w in range(WIDTH):
-                quantise_g(w)
+            quantise_g(0)
+            quantise_g(1)
             regroup_wo(0, "vector")
-            regroup_wo(1, "scalar")
+            quantise_g(2)
             regroup_wo(2, "vector")
+            quantise_g(3)
+            regroup_wo(1, "scalar")
             regroup_wo(3, "scalar")
             transpose_kv(0, 0, 4)
             transpose_kv(0, 1, 5)
@@ -195,23 +199,23 @@ def tile_linear_retention_pb_s_kernel(tc, ret_w, kv_h, Wo, bo, grad_out, out):
                 first_matmul(n)
             copy_kv(0, 0, "scalar")
             copy_kv(0, 1, "vector")
-            copy_go2(0, 0, "scalar")
-            copy_go2(1, 0, "vector")
+            copy_go2(0, 0, 2, "scalar")
+            copy_go2(1, 0, 2, "vector")
             second_matmul(0, 0, 2, 4)
             second_matmul(1, 0, 2, 5)
-            copy_go2(2, 0, "vector")
-            copy_go2(3, 0, "vector")
+            copy_go2(2, 0, 2, "vector")
+            copy_go2(3, 0, 2, "vector")
             copy_kv(1, 0, "scalar")
             second_matmul(0, 2, 2, 6)
             copy_kv(2, 0, "vector")
             second_matmul(1, 2, 2, 7)
             store_out(0, 0, 2, "scalar")
-            copy_go2(0, 1, "scalar")
-            copy_go2(1, 1, "scalar")
+            copy_go2(0, 2, 2, "scalar")
+            copy_go2(1, 2, 2, "scalar")
             second_matmul(2, 0, 2, 4)
             store_out(1, 0, 2, "vector")
-            copy_go2(2, 1, "vector")
-            copy_go2(3, 1, "vector")
+            copy_go2(2, 2, 2, "vector")
+            copy_go2(3, 2, 2, "vector")
             second_matmul(2, 2, 2, 5)
             store_out(0, 2, 2, "scalar")
             second_matmul(3, 0, 2, 6)

@@ -218,12 +218,14 @@ def tile_linear_retention_pb_s_kernel(tc, ret_w, kv_h, Wo, bo, grad_out, out):
             copy_go2(3, 2, 2, "vector")
             second_matmul(2, 2, 2, 5)
             store_out(0, 2, 2, "scalar")
-            second_matmul(3, 0, 2, 6)
             store_out(1, 2, 2, "vector")
-            second_matmul(3, 2, 1, 7)
+            second_matmul(3, 0, 1, 6)
             store_out(2, 0, 2, "scalar")
-            second_matmul(3, 3, 1, 4)
+            second_matmul(3, 1, 1, 7)
             store_out(2, 2, 2, "vector")
-            store_out(3, 0, 2, "scalar")
-            store_out(3, 2, 1, "vector")
-            store_out(3, 3, 1, "scalar")
+            second_matmul(3, 2, 1, 4)
+            store_out(3, 0, 1, "scalar")
+            second_matmul(3, 3, 1, 0)
+            store_out(3, 1, 1, "vector")
+            store_out(3, 2, 1, "scalar")
+            store_out(3, 3, 1, "vector")

@@ -16,7 +16,7 @@ HEIGHT, WIDTH, HEADS, D = 128, 4, 4, 128
 E = P * PACK
 KD = HEADS * D
 TOKENS = HEIGHT * WIDTH
-KV_PIECES = ((0, 2), (2, 1), (3, 1))
+KV_LOADS = ((0, 2), (2, 1), (3, 1))
 IDLE_MATMULS = 2
 
 FLOPS = 2 * TOKENS * E * KD + 2 * WIDTH * HEADS * HEIGHT * D * D
@@ -42,13 +42,14 @@ def tile_linear_retention_pb_s_kernel(tc, ret_w, kv_h, Wo, bo, grad_out, out):
         wo_raw = keep.tile([P, PACK, KD], BF16, name="wo_raw")
         nc.sync.dma_start(out=wo_raw[:], in_=Wo.rearrange("(p t) c -> p t c", t=PACK))
         kv_sb = []
-        for first_w, count in KV_PIECES:
-            kv_piece = keep.tile([P, 4 * count, D], BF16, name="kv_sb%d" % first_w)
+        for first_w, count in KV_LOADS:
+            kv_load = keep.tile([P, count, 4, D], BF16, name="kv_sb%d" % first_w)
             nc.sync.dma_start(
-                out=kv_piece[:],
-                in_=kv_h[0, first_w : first_w + count].rearrange("w n (q l) f -> (w n q) l f", l=4 * count),
+                out=kv_load[:],
+                in_=kv_h[0, first_w : first_w + count].rearrange("w n (q l) f -> (n q) w l f", l=4),
             )
-            kv_sb.append(kv_piece)
+            for i in range(count):
+                kv_sb.append(kv_load[:, i, :, :])
 
         ident_bf16 = keep.tile([P, P], BF16, name="ident_bf16")
         make_identity(nc, ident_bf16[:])
@@ -109,24 +110,21 @@ def tile_linear_retention_pb_s_kernel(tc, ret_w, kv_h, Wo, bo, grad_out, out):
 
         kv_t_banks = {}
         kv_t = []
-        kv_t_of_w = {}
-        for first_w, count in KV_PIECES:
-            kv_t_piece = keep.tile([D, P, 4 * count], F32, name="kv_t%d" % first_w)
-            kv_t.append(kv_t_piece)
-            for i in range(count):
-                kv_t_of_w[first_w + i] = kv_t_piece[:].rearrange("f q l -> f (q l)")[:, i * KD : (i + 1) * KD]
+        for w in range(WIDTH):
+            kv_t_w = keep.tile([D, KD], F32, name="kv_t%d" % w)
+            kv_t.append(kv_t_w)
 
-        def transpose_kv(piece, part, bank):
+        def transpose_kv(w, bank):
             kv_t_ps = psum_bank(bank, [D, 4, P], BF16)
-            for i in range(4):
-                nc.tensor.transpose(kv_t_ps[:, i, :], kv_sb[piece][:, 4 * part + i, :], ident_bf16[:])
-            kv_t_banks[(piece, part)] = kv_t_ps
+            for l in range(4):
+                nc.tensor.transpose(kv_t_ps[:, l, :], kv_sb[w][:, l, :], ident_bf16[:])
+            kv_t_banks[w] = kv_t_ps
 
-        def copy_kv(piece, part, engine):
+        def copy_kv(w, engine):
             copy_on(
                 engine,
-                kv_t[piece][:, :, 4 * part : 4 * part + 4],
-                kv_t_banks[(piece, part)][:].rearrange("f l q -> f q l"),
+                kv_t[w][:].rearrange("f (q l) -> f q l", l=4),
+                kv_t_banks[w][:].rearrange("f l q -> f q l"),
             )
 
         go2_banks = {}
@@ -164,7 +162,7 @@ def tile_linear_retention_pb_s_kernel(tc, ret_w, kv_h, Wo, bo, grad_out, out):
                 nc.tensor.matmul(
                     out=out_ps[:, i, :],
                     lhsT=go2_t[n][:, w * HEIGHT : (w + 1) * HEIGHT],
-                    rhs=kv_t_of_w[w][:, n * D : (n + 1) * D],
+                    rhs=kv_t[w][:, n * D : (n + 1) * D],
                     start=True,
                     stop=True,
                 )
@@ -190,24 +188,24 @@ def tile_linear_retention_pb_s_kernel(tc, ret_w, kv_h, Wo, bo, grad_out, out):
             quantise_g(3)
             regroup_wo(1, "scalar")
             regroup_wo(3, "scalar")
-            transpose_kv(0, 0, 4)
-            transpose_kv(0, 1, 5)
-            transpose_kv(1, 0, 6)
-            transpose_kv(2, 0, 7)
+            for w in range(WIDTH):
+                transpose_kv(w, 4 + w)
             for n in range(HEADS):
                 quantise_wo(n)
                 first_matmul(n)
-            copy_kv(0, 0, "scalar")
-            copy_kv(0, 1, "vector")
-            copy_go2(0, 0, 2, "scalar")
-            copy_go2(1, 0, 2, "vector")
+            copy_kv(0, "scalar")
+            copy_kv(1, "vector")
+            copy_go2(0, 0, 1, "scalar")
+            copy_go2(1, 0, 1, "scalar")
             second_matmul(0, 0, 2, 4)
+            copy_go2(0, 1, 1, "scalar")
+            copy_go2(1, 1, 1, "scalar")
             second_matmul(1, 0, 2, 5)
             copy_go2(2, 0, 2, "vector")
             copy_go2(3, 0, 2, "vector")
-            copy_kv(1, 0, "scalar")
+            copy_kv(2, "scalar")
             second_matmul(0, 2, 2, 6)
-            copy_kv(2, 0, "vector")
+            copy_kv(3, "vector")
             second_matmul(1, 2, 2, 7)
             store_out(0, 0, 2, "scalar")
             copy_go2(0, 2, 2, "scalar")

@@ -16,7 +16,8 @@ HEIGHT, WIDTH, HEADS, D = 128, 4, 4, 128
 E = P * PACK
 KD = HEADS * D
 TOKENS = HEIGHT * WIDTH
-KV_LOADS = ((0, 2), (2, 1), (3, 1))
+KV_PAIRS = WIDTH // 2
+KV_ROWS = 8
 IDLE_MATMULS = 2
 
 FLOPS = 2 * TOKENS * E * KD + 2 * WIDTH * HEADS * HEIGHT * D * D
@@ -42,14 +43,13 @@ def tile_linear_retention_pb_s_kernel(tc, ret_w, kv_h, Wo, bo, grad_out, out):
         wo_raw = keep.tile([P, PACK, KD], BF16, name="wo_raw")
         nc.sync.dma_start(out=wo_raw[:], in_=Wo.rearrange("(p t) c -> p t c", t=PACK))
         kv_sb = []
-        for first_w, count in KV_LOADS:
-            kv_load = keep.tile([P, count, 4, D], BF16, name="kv_sb%d" % first_w)
+        for pair in range(KV_PAIRS):
+            kv_pair = keep.tile([P, KV_ROWS, D], BF16, name="kv_sb%d" % pair)
             nc.sync.dma_start(
-                out=kv_load[:],
-                in_=kv_h[0, first_w : first_w + count].rearrange("w n (q l) f -> (n q) w l f", l=4),
+                out=kv_pair[:],
+                in_=kv_h[0, 2 * pair : 2 * pair + 2].rearrange("w n (q l) f -> (w n q) l f", l=KV_ROWS),
             )
-            for i in range(count):
-                kv_sb.append(kv_load[:, i, :, :])
+            kv_sb.append(kv_pair)
 
         ident_bf16 = keep.tile([P, P], BF16, name="ident_bf16")
         make_identity(nc, ident_bf16[:])
@@ -114,17 +114,18 @@ def tile_linear_retention_pb_s_kernel(tc, ret_w, kv_h, Wo, bo, grad_out, out):
             kv_t_w = keep.tile([D, KD], F32, name="kv_t%d" % w)
             kv_t.append(kv_t_w)
 
-        def transpose_kv(w, bank):
-            kv_t_ps = psum_bank(bank, [D, 4, P], BF16)
-            for l in range(4):
-                nc.tensor.transpose(kv_t_ps[:, l, :], kv_sb[w][:, l, :], ident_bf16[:])
-            kv_t_banks[w] = kv_t_ps
+        def transpose_kv(pair, bank):
+            kv_t_ps = psum_bank(bank, [D, KV_ROWS, P], BF16)
+            for l in range(KV_ROWS):
+                nc.tensor.transpose(kv_t_ps[:, l, :], kv_sb[pair][:, l, :], ident_bf16[:])
+            kv_t_banks[pair] = kv_t_ps
 
         def copy_kv(w, engine):
+            q = slice((w % 2) * (P // 2), (w % 2 + 1) * (P // 2))
             copy_on(
                 engine,
-                kv_t[w][:].rearrange("f (q l) -> f q l", l=4),
-                kv_t_banks[w][:].rearrange("f l q -> f q l"),
+                kv_t[w][:].rearrange("f (q l) -> f q l", l=KV_ROWS),
+                kv_t_banks[w // 2][:, :, q].rearrange("f l q -> f q l"),
             )
 
         go2_banks = {}
@@ -188,8 +189,8 @@ def tile_linear_retention_pb_s_kernel(tc, ret_w, kv_h, Wo, bo, grad_out, out):
             quantise_g(3)
             regroup_wo(1, "scalar")
             regroup_wo(3, "scalar")
-            for w in range(WIDTH):
-                transpose_kv(w, 4 + w)
+            transpose_kv(0, 4)
+            transpose_kv(1, 5)
             for n in range(HEADS):
                 quantise_wo(n)
                 first_matmul(n)
@@ -197,31 +198,31 @@ def tile_linear_retention_pb_s_kernel(tc, ret_w, kv_h, Wo, bo, grad_out, out):
             copy_kv(1, "vector")
             copy_go2(0, 0, 1, "scalar")
             copy_go2(1, 0, 1, "scalar")
-            second_matmul(0, 0, 2, 4)
+            second_matmul(0, 0, 2, 6)
             copy_go2(0, 1, 1, "scalar")
             copy_go2(1, 1, 1, "scalar")
-            second_matmul(1, 0, 2, 5)
+            second_matmul(1, 0, 2, 7)
             copy_go2(2, 0, 2, "vector")
             copy_go2(3, 0, 2, "vector")
             copy_kv(2, "scalar")
-            second_matmul(0, 2, 2, 6)
-            copy_kv(3, "vector")
-            second_matmul(1, 2, 2, 7)
+            second_matmul(0, 2, 2, 4)
             store_out(0, 0, 2, "scalar")
+            copy_kv(3, "vector")
+            second_matmul(1, 2, 2, 6)
             copy_go2(0, 2, 2, "scalar")
             copy_go2(1, 2, 2, "scalar")
-            second_matmul(2, 0, 2, 4)
             store_out(1, 0, 2, "vector")
+            second_matmul(2, 0, 2, 7)
             copy_go2(2, 2, 2, "vector")
             copy_go2(3, 2, 2, "vector")
             second_matmul(2, 2, 2, 5)
             store_out(0, 2, 2, "scalar")
             store_out(1, 2, 2, "vector")
-            second_matmul(3, 0, 1, 6)
+            second_matmul(3, 0, 1, 4)
             store_out(2, 0, 2, "scalar")
-            second_matmul(3, 1, 1, 7)
+            second_matmul(3, 1, 1, 6)
             store_out(2, 2, 2, "vector")
-            second_matmul(3, 2, 1, 4)
+            second_matmul(3, 2, 1, 7)
             store_out(3, 0, 1, "scalar")
             second_matmul(3, 3, 1, 0)
             store_out(3, 1, 1, "vector")

@@ -16,8 +16,7 @@ HEIGHT, WIDTH, HEADS, D = 128, 4, 4, 128
 E = P * PACK
 KD = HEADS * D
 TOKENS = HEIGHT * WIDTH
-KV_PAIRS = WIDTH // 2
-KV_ROWS = 8
+KV_PIECES = ((0, 2), (2, 2))
 IDLE_MATMULS = 2
 
 FLOPS = 2 * TOKENS * E * KD + 2 * WIDTH * HEADS * HEIGHT * D * D
@@ -43,13 +42,13 @@ def tile_linear_retention_pb_s_kernel(tc, ret_w, kv_h, Wo, bo, grad_out, out):
         wo_raw = keep.tile([P, PACK, KD], BF16, name="wo_raw")
         nc.sync.dma_start(out=wo_raw[:], in_=Wo.rearrange("(p t) c -> p t c", t=PACK))
         kv_sb = []
-        for pair in range(KV_PAIRS):
-            kv_pair = keep.tile([P, KV_ROWS, D], BF16, name="kv_sb%d" % pair)
+        for first_w, count in KV_PIECES:
+            kv_piece = keep.tile([P, 4 * count, D], BF16, name="kv_sb%d" % first_w)
             nc.sync.dma_start(
-                out=kv_pair[:],
-                in_=kv_h[0, 2 * pair : 2 * pair + 2].rearrange("w n (q l) f -> (w n q) l f", l=KV_ROWS),
+                out=kv_piece[:],
+                in_=kv_h[0, first_w : first_w + count].rearrange("w n (q l) f -> (w n q) l f", l=4 * count),
             )
-            kv_sb.append(kv_pair)
+            kv_sb.append(kv_piece)
 
         ident_bf16 = keep.tile([P, P], BF16, name="ident_bf16")
         make_identity(nc, ident_bf16[:])
@@ -110,22 +109,25 @@ def tile_linear_retention_pb_s_kernel(tc, ret_w, kv_h, Wo, bo, grad_out, out):
 
         kv_t_banks = {}
         kv_t = []
-        for w in range(WIDTH):
-            kv_t_w = keep.tile([D, KD], F32, name="kv_t%d" % w)
-            kv_t.append(kv_t_w)
+        kv_t_of_w = {}
+        for first_w, count in KV_PIECES:
+            kv_t_piece = keep.tile([D, P, 4 * count], F32, name="kv_t%d" % first_w)
+            kv_t.append(kv_t_piece)
+            for i in range(count):
+                kv_t_of_w[first_w + i] = kv_t_piece[:].rearrange("f q l -> f (q l)")[:, i * KD : (i + 1) * KD]
 
-        def transpose_kv(pair, bank):
-            kv_t_ps = psum_bank(bank, [D, KV_ROWS, P], BF16)
-            for l in range(KV_ROWS):
-                nc.tensor.transpose(kv_t_ps[:, l, :], kv_sb[pair][:, l, :], ident_bf16[:])
-            kv_t_banks[pair] = kv_t_ps
+        def transpose_kv(piece, part, bank):
+            kv_t_ps = psum_bank(bank, [D, 4, P], BF16)
+            for i in range(4):
+                nc.tensor.transpose(kv_t_ps[:, i, :], kv_sb[piece][:, 4 * part + i, :], ident_bf16[:])
+            kv_t_banks[(piece, part)] = kv_t_ps
 
-        def copy_kv(w, engine):
-            q = slice((w % 2) * (P // 2), (w % 2 + 1) * (P // 2))
+        def copy_kv(piece, part, i, engine):
+            q = slice(i * (P // 2), (i + 1) * (P // 2))
             copy_on(
                 engine,
-                kv_t[w][:].rearrange("f (q l) -> f q l", l=KV_ROWS),
-                kv_t_banks[w // 2][:, :, q].rearrange("f l q -> f q l"),
+                kv_t[piece][:, q, 4 * part : 4 * part + 4],
+                kv_t_banks[(piece, part)][:, :, q].rearrange("f l q -> f q l"),
             )
 
         go2_banks = {}
@@ -163,7 +165,7 @@ def tile_linear_retention_pb_s_kernel(tc, ret_w, kv_h, Wo, bo, grad_out, out):
                 nc.tensor.matmul(
                     out=out_ps[:, i, :],
                     lhsT=go2_t[n][:, w * HEIGHT : (w + 1) * HEIGHT],
-                    rhs=kv_t[w][:, n * D : (n + 1) * D],
+                    rhs=kv_t_of_w[w][:, n * D : (n + 1) * D],
                     start=True,
                     stop=True,
                 )
@@ -189,40 +191,46 @@ def tile_linear_retention_pb_s_kernel(tc, ret_w, kv_h, Wo, bo, grad_out, out):
             quantise_g(3)
             regroup_wo(1, "scalar")
             regroup_wo(3, "scalar")
-            transpose_kv(0, 4)
-            transpose_kv(1, 5)
+            transpose_kv(0, 0, 4)
+            transpose_kv(0, 1, 5)
+            transpose_kv(1, 0, 6)
+            transpose_kv(1, 1, 7)
             for n in range(HEADS):
                 quantise_wo(n)
                 first_matmul(n)
-            copy_kv(0, "scalar")
-            copy_kv(1, "vector")
+            copy_kv(0, 0, 0, "scalar")
+            copy_kv(0, 0, 1, "scalar")
+            copy_kv(0, 1, 0, "vector")
+            copy_kv(0, 1, 1, "vector")
             copy_go2(0, 0, 1, "scalar")
             copy_go2(1, 0, 1, "scalar")
-            second_matmul(0, 0, 2, 6)
+            second_matmul(0, 0, 2, 4)
             copy_go2(0, 1, 1, "scalar")
             copy_go2(1, 1, 1, "scalar")
-            second_matmul(1, 0, 2, 7)
+            second_matmul(1, 0, 2, 5)
             copy_go2(2, 0, 2, "vector")
             copy_go2(3, 0, 2, "vector")
-            copy_kv(2, "scalar")
-            second_matmul(0, 2, 2, 4)
+            copy_kv(1, 0, 0, "scalar")
+            copy_kv(1, 0, 1, "scalar")
+            second_matmul(0, 2, 2, 6)
+            copy_kv(1, 1, 0, "vector")
+            copy_kv(1, 1, 1, "vector")
+            second_matmul(1, 2, 2, 7)
             store_out(0, 0, 2, "scalar")
-            copy_kv(3, "vector")
-            second_matmul(1, 2, 2, 6)
             copy_go2(0, 2, 2, "scalar")
             copy_go2(1, 2, 2, "scalar")
+            second_matmul(2, 0, 2, 4)
             store_out(1, 0, 2, "vector")
-            second_matmul(2, 0, 2, 7)
             copy_go2(2, 2, 2, "vector")
             copy_go2(3, 2, 2, "vector")
             second_matmul(2, 2, 2, 5)
             store_out(0, 2, 2, "scalar")
             store_out(1, 2, 2, "vector")
-            second_matmul(3, 0, 1, 4)
+            second_matmul(3, 0, 1, 6)
             store_out(2, 0, 2, "scalar")
-            second_matmul(3, 1, 1, 6)
+            second_matmul(3, 1, 1, 7)
             store_out(2, 2, 2, "vector")
-            second_matmul(3, 2, 1, 7)
+            second_matmul(3, 2, 1, 4)
             store_out(3, 0, 1, "scalar")
             second_matmul(3, 3, 1, 0)
             store_out(3, 1, 1, "vector")

from contextlib import ExitStack

import concourse.mybir as mybir
from concourse.masks import make_identity

BF16 = mybir.dt.bfloat16
F32 = mybir.dt.float32
U32 = mybir.dt.uint32
U8 = mybir.dt.uint8
E4M3_X4 = mybir.dt.float8_e4m3fn_x4
E5M2_X4 = mybir.dt.float8_e5m2_x4

P = 128
PACK = 4
HEIGHT, WIDTH, HEADS, D = 128, 4, 4, 128
E = P * PACK
KD = HEADS * D
TOKENS = HEIGHT * WIDTH
KV_PIECES = ((0, 2), (2, 2))
IDLE_MATMULS = 2

FLOPS = 2 * TOKENS * E * KD + 2 * WIDTH * HEADS * HEIGHT * D * D
BYTES = 2 * (TOKENS * E + E * KD + WIDTH * HEADS * D * D) + 4 * TOKENS * KD


def tile_linear_retention_pb_s_kernel(tc, ret_w, kv_h, Wo, bo, grad_out, out):
    nc = tc.nc
    with ExitStack() as ctx:
        keep = ctx.enter_context(tc.tile_pool(name="keep", bufs=1))
        psum = ctx.enter_context(tc.psum_pool(name="psum", bufs=1))

        def psum_bank(bank, shape, dtype):
            in_bank = psum.tile(shape, dtype, tag="bank%d" % bank)
            return in_bank

        g_rows = grad_out[0].rearrange("(h w) k -> h w k", w=WIDTH)
        g_sb = []
        for pair in range(WIDTH // 2):
            g_pair = keep.tile([HEIGHT, 2, E], BF16, name="g_sb%d" % pair)
            nc.sync.dma_start(out=g_pair[:], in_=g_rows[:, 2 * pair : 2 * pair + 2, :])
            g_sb.append(g_pair)
        wo_raw = keep.tile([P, PACK, KD], BF16, name="wo_raw")
        nc.sync.dma_start(out=wo_raw[:], in_=Wo.rearrange("(p t) c -> p t c", t=PACK))
        kv_sb = []
        for first_w, count in KV_PIECES:
            kv_piece = keep.tile([P, 4 * count, D], BF16, name="kv_sb%d" % first_w)
            nc.sync.dma_start(
                out=kv_piece[:],
                in_=kv_h[0, first_w : first_w + count].rearrange("w n (q l) f -> (w n q) l f", l=4 * count),
            )
            kv_sb.append(kv_piece)

        ident_bf16 = keep.tile([P, P], BF16, name="ident_bf16")
        make_identity(nc, ident_bf16[:])
        ident_f32 = keep.tile([P, P], F32, name="ident_f32")
        make_identity(nc, ident_f32[:])

        def copy_on(engine, out_ap, in_ap):
            if engine == "vector":
                nc.vector.tensor_copy(out=out_ap, in_=in_ap)
            else:
                nc.scalar.copy(out=out_ap, in_=in_ap)

        g_codes = keep.tile([P, TOKENS], U32, name="g_codes", align_bytes=64)
        g_scales = keep.tile([P, TOKENS], U8, name="g_scales", align_bytes=64)
        wo_grouped = keep.tile([P, KD, PACK], BF16, name="wo_grouped", align_bytes=64)
        wo_codes = keep.tile([P, KD], U32, name="wo_codes", align_bytes=64)
        wo_scales = keep.tile([P, KD], U8, name="wo_scales", align_bytes=64)

        g_grouped = []

        def transpose_g(w, engine):
            words = g_sb[w // 2][:, w % 2, :].bitcast(F32).rearrange("h (p u) -> h u p", u=2)
            g_t = psum_bank(w, [P, 2, HEIGHT], F32)
            for u in range(2):
                nc.tensor.transpose(g_t[:, u, :], words[:, u, :], ident_f32[:])
            grouped = keep.tile([P, HEIGHT, PACK], BF16, name="g_grouped%d" % w, align_bytes=64)
            copy_on(engine, grouped[:].bitcast(F32), g_t[:].rearrange("p u h -> p h u"))
            g_grouped.append(grouped)

        def idle_matmuls(count):
            idle_ps = psum_bank(7, [P, P], F32)
            for i in range(count):
                nc.tensor.matmul(out=idle_ps[:], lhsT=ident_f32[:], rhs=ident_f32[:], start=True, stop=True)

        def quantise_g(w):
            cols = slice(w * HEIGHT, (w + 1) * HEIGHT)
            nc.vector.quantize_mx(
                out=g_codes[:, cols].bitcast(E5M2_X4),
                scales=g_scales[:, cols],
                in_=g_grouped[w][:].rearrange("p h t -> p (h t)"),
            )

        def regroup_wo(n, engine):
            cols = slice(n * D, (n + 1) * D)
            copy_on(
                engine,
                wo_grouped[:, cols, :].rearrange("p (c i) t -> p c t i", i=4),
                wo_raw[:, :, cols].rearrange("p t (c i) -> p c t i", i=4),
            )

        def quantise_wo(n):
            cols = slice(n * D, (n + 1) * D)
            nc.vector.quantize_mx(
                out=wo_codes[:, cols].bitcast(E4M3_X4),
                scales=wo_scales[:, cols],
                in_=wo_grouped[:, cols, :].rearrange("p c t -> p (c t)"),
            )

        kv_t_banks = {}
        kv_t = []
        kv_t_of_w = {}
        for first_w, count in KV_PIECES:
            kv_t_piece = keep.tile([D, P, 4 * count], F32, name="kv_t%d" % first_w)
            kv_t.append(kv_t_piece)
            for i in range(count):
                kv_t_of_w[first_w + i] = kv_t_piece[:].rearrange("f q l -> f (q l)")[:, i * KD : (i + 1) * KD]

        def transpose_kv(piece, part, bank):
            kv_t_ps = psum_bank(bank, [D, 4, P], BF16)
            for i in range(4):
                nc.tensor.transpose(kv_t_ps[:, i, :], kv_sb[piece][:, 4 * part + i, :], ident_bf16[:])
            kv_t_banks[(piece, part)] = kv_t_ps

        def copy_kv(piece, part, i, engine):
            q = slice(i * (P // 2), (i + 1) * (P // 2))
            copy_on(
                engine,
                kv_t[piece][:, q, 4 * part : 4 * part + 4],
                kv_t_banks[(piece, part)][:, :, q].rearrange("f l q -> f q l"),
            )

        go2_banks = {}
        go2_t = {}

        def first_matmul(n):
            cols = slice(n * D, (n + 1) * D)
            go2_ps = psum_bank(n, [D, TOKENS], F32)
            nc.tensor.matmul_mx(
                out=go2_ps[:],
                lhsT=wo_codes[:, cols].bitcast(E4M3_X4),
                lhsT_scale=wo_scales[:, cols],
                rhs=g_codes[:].bitcast(E5M2_X4),
                rhs_scale=g_scales[:],
                start=True,
                stop=True,
            )
            go2_banks[n] = go2_ps

        for n in range(HEADS):
            go2_n = keep.tile([D, TOKENS], F32, name="go2_t%d" % n)
            go2_t[n] = go2_n

        def copy_go2(n, first_w, count, engine):
            cols = slice(first_w * HEIGHT, (first_w + count) * HEIGHT)
            copy_on(engine, go2_t[n][:, cols], go2_banks[n][:, cols])

        out_sb = keep.tile([HEIGHT, WIDTH, HEADS, D], F32, name="out_sb")
        out_banks = {}

        def second_matmul(w, first_head, heads, bank):
            out_ps = psum_bank(bank, [HEIGHT, heads, D], F32)
            for i in range(heads):
                n = first_head + i
                nc.tensor.matmul(
                    out=out_ps[:, i, :],
                    lhsT=go2_t[n][:, w * HEIGHT : (w + 1) * HEIGHT],
                    rhs=kv_t_of_w[w][:, n * D : (n + 1) * D],
                    start=True,
                    stop=True,
                )
            out_banks[(w, first_head)] = out_ps

        def store_out(w, first_head, heads, engine):
            which = slice(first_head, first_head + heads)
            copy_on(engine, out_sb[:, w, which, :], out_banks[(w, first_head)][:])
            nc.sync.dma_start(out=out[0, :, w, which, :], in_=out_sb[:, w, which, :])

        with tc.manual_schedule():
            idle_matmuls(IDLE_MATMULS)
            transpose_g(0, "scalar")
            transpose_g(1, "vector")
            transpose_g(2, "scalar")
            transpose_g(3, "scalar")
            idle_matmuls(IDLE_MATMULS)
            quantise_g(0)
            quantise_g(1)
            regroup_wo(0, "vector")
            quantise_g(2)
            regroup_wo(2, "vector")
            quantise_g(3)
            regroup_wo(1, "scalar")
            regroup_wo(3, "scalar")
            transpose_kv(0, 0, 4)
            transpose_kv(0, 1, 5)
            transpose_kv(1, 0, 6)
            transpose_kv(1, 1, 7)
            for n in range(HEADS):
                quantise_wo(n)
                first_matmul(n)
            copy_kv(0, 0, 0, "scalar")
            copy_kv(0, 0, 1, "scalar")
            copy_kv(0, 1, 0, "vector")
            copy_kv(0, 1, 1, "vector")
            copy_go2(0, 0, 1, "scalar")
            copy_go2(1, 0, 1, "scalar")
            second_matmul(0, 0, 2, 4)
            copy_go2(0, 1, 1, "scalar")
            copy_go2(1, 1, 1, "scalar")
            second_matmul(1, 0, 2, 5)
            copy_go2(2, 0, 2, "vector")
            copy_go2(3, 0, 2, "vector")
            copy_kv(1, 0, 0, "scalar")
            copy_kv(1, 0, 1, "scalar")
            second_matmul(0, 2, 2, 6)
            copy_kv(1, 1, 0, "vector")
            copy_kv(1, 1, 1, "vector")
            second_matmul(1, 2, 2, 7)
            store_out(0, 0, 2, "scalar")
            copy_go2(0, 2, 2, "scalar")
            copy_go2(1, 2, 2, "scalar")
            second_matmul(2, 0, 2, 4)
            store_out(1, 0, 2, "vector")
            copy_go2(2, 2, 2, "vector")
            copy_go2(3, 2, 2, "vector")
            second_matmul(2, 2, 2, 5)
            store_out(0, 2, 2, "scalar")
            store_out(1, 2, 2, "vector")
            second_matmul(3, 0, 1, 6)
            store_out(2, 0, 2, "scalar")
            second_matmul(3, 1, 1, 7)
            store_out(2, 2, 2, "vector")
            second_matmul(3, 2, 1, 4)
            store_out(3, 0, 1, "scalar")
            second_matmul(3, 3, 1, 0)
            store_out(3, 1, 1, "vector")
            store_out(3, 2, 1, "scalar")
            store_out(3, 3, 1, "vector")
